import numpy as np
import ml_dtypes


def mxq(x, axis, fmt="e4m3"):
    dtype, down = {"e4m3": (ml_dtypes.float8_e4m3fn, 7), "e5m2": (ml_dtypes.float8_e5m2, 14)}[fmt]
    v = np.moveaxis(np.asarray(x, np.float32).astype(ml_dtypes.bfloat16).astype(np.float64), axis, -1)
    blocks = v.reshape(v.shape[:-1] + (-1, 32))
    amax = np.abs(blocks).max(-1, keepdims=True)
    byte = np.maximum(np.where(amax > 0, np.frexp(amax)[1] - 1 + 127, 0) - down, 1)
    scale = np.exp2(byte - 127.0)
    codes = (blocks / scale).astype(np.float32).astype(dtype).astype(np.float64)
    return np.moveaxis((codes * scale).reshape(v.shape), -1, axis)


WIDE = False


def mx_kscale(k):
    if not WIDE:
        return np.ones(k)
    levels = np.array([10, -10, 5, -5, 0])
    if k % 512:
        return np.exp2(np.random.permutation(np.resize(levels, k // 32))).repeat(32)
    a = np.empty((k // 512, 16))
    for p in range(k // 512):
        a[p, :8] = np.random.permutation(np.resize(levels, 8))
        for g in range(8):
            far = levels[np.abs(levels - a[p, g]) >= 10]
            a[p, g + 8] = far[np.random.randint(len(far))]
    return np.exp2(a.ravel()).repeat(32)


BF16 = ml_dtypes.bfloat16


def bf(x):
    return np.asarray(x, np.float32).astype(BF16)


def f64(x):
    return np.asarray(x).astype(np.float64)


E2M1 = np.array([0.0, 0.5, 1.0, 1.5, 2.0, 3.0, 4.0, 6.0, -0.0, -0.5, -1.0, -1.5, -2.0, -3.0, -4.0, -6.0])


def pack_weight(w, fmt):
    k, n = w.shape
    w = f64(bf(w)).reshape(k // 32, 32, n)
    amax = np.abs(w).max(1)
    if fmt == "e4m3":
        byte = np.frexp(amax)[1] - 1 + 127 - 7
    else:
        mant, ex = np.frexp(amax / 6.0)
        byte = np.where(mant > 0.5, ex, ex - 1) + 127
    byte = np.clip(np.where(amax > 0, byte, 1), 1, 254)
    scaled = (w * np.exp2(127.0 - byte)[:, None, :]).reshape(k, n).astype(np.float32)
    by_word = np.ascontiguousarray(scaled.reshape(k // 512, 128, 4, n).transpose(0, 1, 3, 2))
    if fmt == "e4m3":
        words = by_word.astype(ml_dtypes.float8_e4m3fn).view(np.uint8)
    else:
        c = by_word.astype(ml_dtypes.float4_e2m1fn).view(np.uint8) & 0xF
        words = c[..., 0::2] | (c[..., 1::2] << 4)
    return np.ascontiguousarray(words), np.ascontiguousarray(byte.astype(np.uint8).reshape(k // 512, 16, n))


def unpack_weight(words, scales, fmt):
    g, p, n, _ = words.shape
    if fmt == "e4m3":
        vals = np.ascontiguousarray(words).view(ml_dtypes.float8_e4m3fn).astype(np.float64)
    else:
        nib = np.empty((g, p, n, 4), np.uint8)
        nib[..., 0::2] = words & 0xF
        nib[..., 1::2] = words >> 4
        vals = E2M1[nib]
    vals = vals * np.repeat(np.exp2(scales.astype(np.float64) - 127.0), 8, axis=1)[..., None]
    return vals.transpose(0, 1, 3, 2).reshape(g * 512, n)
def pack4(w):
    words, scales = pack_weight(w, "e2m1")
    return words.reshape(words.shape[0], 128, -1), scales


def unpack4(words, scales):
    return unpack_weight(words.reshape(words.shape[0], 128, -1, 2), scales, "e2m1")


B, T, D, NH, N_MLP = 4, 1024, 512, 16, 512
LN_EPS = 1e-6


def layer_norm(v, g, b):
    mu = v.mean(-1, keepdims=True)
    var = np.square(v - mu).mean(-1, keepdims=True)
    return (v - mu) / np.sqrt(var + LN_EPS) * g + b


def erf(v):
    z = np.clip(v, -6.0, 6.0)
    r = 2.0 * z * z
    term = z.copy()
    total = z.copy()
    for n in range(1, 120):
        term = term * r / (2.0 * n + 1.0)
        total = total + term
    return 2.0 / np.sqrt(np.pi) * np.exp(-z * z) * total


def gelu_erf(v):
    return 0.5 * v * (1.0 + erf(v / np.sqrt(2.0)))


def draw0():
    s, t = mx_kscale(D), mx_kscale(D)
    attn_out = bf(np.random.standard_normal((B, T, D)) * 0.25 * s)
    x = bf(np.random.standard_normal((B, T, D)) * 1.5 + np.random.standard_normal((B, T, 1)) * 0.5)
    W_proj_words, W_proj_scales = pack4((np.random.standard_normal((D, D)) * 3.0 / np.sqrt(D) / s).T)
    b_proj = bf(np.random.standard_normal(D) * 0.2)
    g2 = bf((1.0 + 0.1 * np.random.standard_normal(D)) * t)
    beta2 = bf(0.1 * np.random.standard_normal(D) * t)
    W1_words, W1_scales = pack4((np.random.standard_normal((N_MLP, D)) / np.sqrt(D) / t).T)
    b1 = bf(np.random.standard_normal(N_MLP) * 0.2)
    return {"attn_out": attn_out,
            "x": x,
            "W_proj_words": W_proj_words,
            "W_proj_scales": W_proj_scales,
            "b_proj": b_proj,
            "g2": g2,
            "beta2": beta2,
            "W1_words": W1_words,
            "W1_scales": W1_scales,
            "b1": b1}


def core(attn_out, x, W_proj_words, W_proj_scales, b_proj, g2, beta2, W1_words, W1_scales, b1):
    o = (mxq(f64(attn_out), 2, "e4m3") @ unpack4(W_proj_words, W_proj_scales)) + f64(b_proj)
    x_mid = f64(x) + o
    h = layer_norm(x_mid, f64(g2), f64(beta2))
    u = gelu_erf((mxq(h, 2, "e4m3") @ unpack4(W1_words, W1_scales)) + f64(b1))
    return x_mid, u


def e4m3fn_bytes(y):
    return np.clip(np.asarray(y, np.float64), -448.0, 448.0).astype(np.float32).astype(ml_dtypes.float8_e4m3fn).view(np.uint8)


def e4m3fn_values(b):
    return np.asarray(b, np.uint8).view(ml_dtypes.float8_e4m3fn).astype(np.float64)


def setup_inputs():
    d = draw0()
    x0 = np.asarray(d['attn_out']).astype(np.float64)
    s = (np.max(np.abs(x0), axis=(0, 1), keepdims=True) / 448.0).astype(np.float32)
    out = {}
    for k, v in d.items():
        if k == 'attn_out':
            out['attn_out_bytes'] = e4m3fn_bytes(x0 / s.astype(np.float64))
            out['attn_out_scale'] = s
        else:
            out[k] = v
    return out


def reference(attn_out_bytes, attn_out_scale, x, W_proj_words, W_proj_scales, b_proj, g2, beta2, W1_words, W1_scales, b1):
    return core(e4m3fn_values(attn_out_bytes) * attn_out_scale.astype(np.float64), x, W_proj_words, W_proj_scales, b_proj, g2, beta2, W1_words, W1_scales, b1)

from contextlib import ExitStack

import concourse.mybir as mybir
from concourse.masks import make_identity

F32 = mybir.dt.float32
BF16 = mybir.dt.bfloat16
U32 = mybir.dt.uint32
I32 = mybir.dt.int32
U8 = mybir.dt.uint8
FP8 = mybir.dt.float8_e4m3fn
FP8X4 = mybir.dt.float8_e4m3fn_x4
FP4X4 = mybir.dt.float4_e2m1fn_x4
ALU = mybir.AluOpType
ACT = mybir.ActivationFunctionType

P = 128
TOKENS = 4096
D = 512
N_TILES = TOKENS // P
PACK = 4
BANK = 512
LN_EPS = 1e-6
FLOPS = 2 * 2 * TOKENS * D * D

GROUPS = [(0, 1), (1, 1)] + [(i, 2) for i in range(2, 30, 2)] + [(30, 1), (31, 1)]
BYTE_CHUNKS = [(0, 2), (2, 8), (8, 16), (16, 24), (24, 32)]
X_CHUNKS = [(0, 2), (2, 4), (4, 8), (8, 12), (12, 16), (16, 20), (20, 24), (24, 28), (28, 32)]
SCHEDULE = [("mm2", 8), ("turn2", 6), ("product", 0), ("quant1", 1), ("affine", 6), ("turn1", 0), ("inter", 7), ("mid", 4), ("quant2", 7), ("copy1", 0), ("square", 4), ("mm1", 1), ("bias", 8), ("zb", 1), ("turnb", 3), ("small", 5), ("gelu", 8), ("norm", 5)]


def tile_block_pb_t_w4_kernel(tc, attn_out_bytes, attn_out_scale, x, W_proj_words, W_proj_scales, b_proj, g2, beta2, W1_words, W1_scales, b1, out_0, out_1):
    nc = tc.nc
    bytes_hbm = attn_out_bytes.rearrange("b (q i) d -> (b q) (i d)", i=N_TILES)
    x_hbm = x.rearrange("b (q i) d -> (b q) (i d)", i=N_TILES)
    mid_hbm = out_0.rearrange("b (q i) d -> (b q) (i d)", i=N_TILES)
    u_hbm = out_1.rearrange("b (q i) d -> (b q) (i d)", i=N_TILES)

    with ExitStack() as ctx:
        const = ctx.enter_context(tc.tile_pool(name="const", bufs=1))
        work = ctx.enter_context(tc.tile_pool(name="work", bufs=2))
        psum = ctx.enter_context(tc.psum_pool(name="psum", bufs=8))
        ctx.enter_context(tc.manual_schedule())

        scale2 = const.tile([P, 2 * D], F32)
        nc.scalar.dma_start(out=scale2[:, 0:D], in_=attn_out_scale.rearrange("a b k -> (a b k)").partition_broadcast(P))
        ident = const.tile([P, P], F32)
        make_identity(nc, ident[:])
        warm = const.tile([P, 1], F32)
        nc.vector.memset(warm[:], 0.0)
        nc.scalar.activation(out=warm[:], in_=warm[:], func=ACT.Gelu)
        bp_rows = const.tile([P, P], BF16)
        nc.vector.memset(bp_rows[:], 0.0)
        nc.scalar.dma_start(out=bp_rows[0:PACK, :], in_=b_proj.rearrange("(t p) -> t p", p=P))
        g_cols_bf = const.tile([P, PACK], BF16)
        nc.scalar.dma_start(out=g_cols_bf[:], in_=g2.rearrange("(p t) -> p t", t=PACK))
        beta_cols_bf = const.tile([P, PACK], BF16)
        nc.scalar.dma_start(out=beta_cols_bf[:], in_=beta2.rearrange("(p t) -> p t", t=PACK))
        b1_row = const.tile([P, D], BF16)
        nc.gpsimd.dma_start(out=b1_row[:], in_=b1.partition_broadcast(P))

        byte_tiles = []
        x_tiles = []

        def load_bytes(c):
            lo, hi = BYTE_CHUNKS[c]
            code_bytes = const.tile([P, (hi - lo) * D], U8, name="code_bytes%d" % c, align_bytes=64)
            nc.sync.dma_start(out=code_bytes[:], in_=bytes_hbm[:, lo * D : hi * D])
            byte_tiles.append(code_bytes)

        def load_x(c):
            lo, hi = X_CHUNKS[c]
            xt = const.tile([P, (hi - lo) * D], BF16, name="xt%d" % c)
            nc.sync.dma_start(out=xt[:], in_=x_hbm[:, lo * D : hi * D])
            x_tiles.append(xt)

        wp = const.tile([P, 2 * D], U8, align_bytes=64)
        w1 = const.tile([P, 2 * D], U8, align_bytes=64)
        wp_scales = const.tile([P, D], U8, align_bytes=64)
        w1_scales = const.tile([P, D], U8, align_bytes=64)
        nc.vector.memset(wp_scales[:].bitcast(I32), 0)
        nc.vector.memset(w1_scales[:].bitcast(I32), 0)

        load_bytes(0)
        nc.sync.dma_start(out=wp[:].bitcast(I32), in_=W_proj_words[0].bitcast(I32))
        for dst, src in ((wp_scales, W_proj_scales), (w1_scales, W1_scales)):
            for q in range(4):
                nc.sync.dma_start(out=dst[32 * q : 32 * q + 4, :].bitcast(I32), in_=src[0, 4 * q : 4 * q + 4, :].bitcast(I32))
        load_bytes(1)
        load_x(0)
        load_x(1)
        nc.sync.dma_start(out=w1[:].bitcast(I32), in_=W1_words[0].bitcast(I32))
        load_x(2)
        load_bytes(2)
        load_x(3)
        load_x(4)
        for c in (3, 4):
            load_bytes(c)
            load_x(2 * c - 1)
            load_x(2 * c)

        minus_half = const.tile([P, 2], F32)
        nc.gpsimd.memset(minus_half[:], -0.5)
        bp_rows_f = const.tile([P, P], F32)
        nc.gpsimd.tensor_copy(out=bp_rows_f[:], in_=bp_rows[:])
        g_cols = const.tile([P, PACK], F32)
        nc.gpsimd.tensor_copy(out=g_cols[:], in_=g_cols_bf[:])
        beta_cols = const.tile([P, PACK], F32)
        nc.gpsimd.tensor_copy(out=beta_cols[:], in_=beta_cols_bf[:])
        bp_turn = psum.tile([P, BANK], F32, name="bank")
        nc.tensor.transpose(bp_turn[:, 0:P], bp_rows_f[:], ident[:])
        bp_cols = const.tile([P, PACK], F32)
        nc.scalar.copy(out=bp_cols[:], in_=bp_turn[:, 0:PACK])
        nc.vector.tensor_copy(out=scale2[:, D : 2 * D], in_=scale2[:, 0:D])

        def chunk_of(chunks, tiles, first):
            for (lo, hi), t in zip(chunks, tiles):
                if lo <= first < hi:
                    return t, first - lo
            raise ValueError("no chunk")

        n_groups = len(GROUPS)
        st = [dict() for g in range(n_groups)]

        def product(g):
            first, n = GROUPS[g]
            t, off = chunk_of(BYTE_CHUNKS, byte_tiles, first)
            prod = work.tile([P, n * D], BF16, name="prod", align_bytes=64, bufs=3)
            nc.vector.tensor_tensor(out=prod[:], in0=t[:, off * D : (off + n) * D].bitcast(FP8), in1=scale2[:, 0 : n * D], op=ALU.mult)
            st[g]["prod"] = prod

        def turn1(g):
            n = GROUPS[g][1]
            bank = psum.tile([P, BANK], F32, name="bank")
            words = st[g]["prod"][:].bitcast(F32)
            for i in range(n):
                for u in range(2):
                    nc.tensor.transpose(bank[:, (2 * i + u) * P : (2 * i + u + 1) * P], words[:, 256 * i + u : 256 * (i + 1) : 2], ident[:])
            st[g]["turn1"] = bank

        def copy1(g):
            n = GROUPS[g][1]
            grp = work.tile([P, n * D], BF16, name="grp1", align_bytes=64)
            nc.scalar.copy(out=grp[:].bitcast(F32).rearrange("p (i r u) -> p i r u", i=n, u=2), in_=st[g]["turn1"][:, 0 : 2 * n * P].rearrange("p (i u r) -> p i r u", i=n, u=2))
            st[g]["grp1"] = grp

        def quantize(grp, n, tag):
            codes = work.tile([P, n * P], U32, name="codes" + tag, align_bytes=64)
            scales = work.tile([P, n * P], U8, name="scales" + tag, align_bytes=64)
            nc.vector.quantize_mx(out=codes[:].bitcast(FP8X4), scales=scales[:], in_=grp[:])
            return codes, scales

        def quant1(g):
            st[g]["q1"] = quantize(st[g]["grp1"], GROUPS[g][1], "1")

        def mm1(g):
            n = GROUPS[g][1]
            codes, scales = st[g]["q1"]
            banks = [psum.tile([P, BANK], F32, name="bank") for b in range(n)]
            accs = []
            for t in range(PACK):
                at = t * n * P
                acc = banks[at // BANK][:, at % BANK : at % BANK + n * P]
                nc.tensor.matmul_mx(
                    out=acc,
                    lhsT=wp[:, 2 * t * P : 2 * (t + 1) * P].bitcast(FP4X4),
                    lhsT_scale=wp_scales[:, t * P : (t + 1) * P],
                    rhs=codes[:].bitcast(FP8X4),
                    rhs_scale=scales[:],
                    start=True,
                    stop=True,
                )
                accs.append(acc)
            st[g]["acc1"] = accs

        def zb(g):
            n = GROUPS[g][1]
            z = work.tile([P, PACK, n * P], F32, name="z")
            for t in range(PACK):
                nc.scalar.activation(out=z[:, t, :], in_=st[g]["acc1"][t], func=ACT.Identity, bias=bp_cols[:, t : t + 1])
            st[g]["z"] = z

        def turnb(g):
            n = GROUPS[g][1]
            banks = []
            for i in range(n):
                bank = psum.tile([P, BANK], F32, name="bank")
                for t in range(PACK):
                    nc.tensor.transpose(bank[:, t * P : (t + 1) * P], st[g]["z"][:, t, i * P : (i + 1) * P], ident[:])
                banks.append(bank)
            st[g]["turnb"] = banks

        def mid(g):
            first, n = GROUPS[g]
            t, off = chunk_of(X_CHUNKS, x_tiles, first)
            mid = work.tile([P, n, D], F32, name="mid", bufs=6)
            sums = work.tile([P, n], F32, name="sums", bufs=6)
            for i in range(n):
                nc.vector.scalar_tensor_tensor(out=mid[:, i, :], in0=st[g]["turnb"][i][:], scalar=1.0, in1=t[:, (off + i) * D : (off + i + 1) * D], op0=ALU.mult, op1=ALU.add, accum_out=sums[:, i : i + 1])
            nc.sync.dma_start(out=mid_hbm[:, first * D : (first + n) * D], in_=mid[:].rearrange("p i d -> p (i d)"))
            st[g]["mid"] = mid
            st[g]["sums"] = sums

        def square(g):
            n = GROUPS[g][1]
            ssq = work.tile([P, n], F32, name="ssq", bufs=6)
            for i in range(n):
                junk = work.tile([P, D], BF16, name="junk")
                nc.scalar.activation(out=junk[:], in_=st[g]["mid"][:, i, :], func=ACT.Square, scale=-float(D), bias=st[g]["sums"][:, i : i + 1], accum_out=ssq[:, i : i + 1])
            st[g]["ssq"] = ssq

        def small(g):
            n = GROUPS[g][1]
            nmean = work.tile([P, n], F32, name="nmean", bufs=6)
            nc.gpsimd.tensor_scalar(out=nmean[:], in0=st[g]["sums"][:], scalar1=-1.0 / D, scalar2=0.0, op0=ALU.mult, op1=ALU.add)
            var = work.tile([P, n], F32, name="var", bufs=6)
            nc.gpsimd.tensor_scalar(out=var[:], in0=st[g]["ssq"][:], scalar1=1.0 / D**3, scalar2=LN_EPS, op0=ALU.mult, op1=ALU.add)
            rstd = work.tile([P, n], F32, name="rstd", bufs=6)
            nc.gpsimd.tensor_tensor(out=rstd[:], in0=var[:], in1=minus_half[:, 0:n], op=ALU.pow)
            shift = work.tile([P, n], F32, name="shift", bufs=6)
            nc.gpsimd.tensor_tensor(out=shift[:], in0=nmean[:], in1=rstd[:], op=ALU.mult)
            st[g]["rstd"] = rstd
            st[g]["shift"] = shift

        def norm(g):
            n = GROUPS[g][1]
            xn = work.tile([P, n, D], F32, name="xn")
            for i in range(n):
                nc.vector.tensor_scalar(out=xn[:, i, :], in0=st[g]["mid"][:, i, :], scalar1=st[g]["rstd"][:, i : i + 1], scalar2=st[g]["shift"][:, i : i + 1], op0=ALU.mult, op1=ALU.add)
            st[g]["xn"] = xn

        def turn2(g):
            n = GROUPS[g][1]
            banks = [psum.tile([P, BANK], F32, name="bank") for b in range(n)]
            planes = []
            for t in range(PACK):
                at = t * n * P
                plane = banks[at // BANK][:, at % BANK : at % BANK + n * P]
                for i in range(n):
                    nc.tensor.transpose(plane[:, i * P : (i + 1) * P], st[g]["xn"][:, i, t:D:PACK], ident[:])
                planes.append(plane)
            st[g]["turn2"] = planes

        def affine(g):
            n = GROUPS[g][1]
            planes = work.tile([P, PACK, n * P], BF16, name="planes")
            for t in range(PACK):
                nc.scalar.activation(out=planes[:, t, :], in_=st[g]["turn2"][t], func=ACT.Identity, scale=g_cols[:, t : t + 1], bias=beta_cols[:, t : t + 1])
            st[g]["planes"] = planes

        def inter(g):
            n = GROUPS[g][1]
            grp = work.tile([P, n * D], BF16, name="grp2", align_bytes=64)
            nc.vector.tensor_copy(out=grp[:].rearrange("p (c i t) -> p c t i", i=4, t=PACK), in_=st[g]["planes"][:].rearrange("p t (c i) -> p c t i", i=4))
            st[g]["grp2"] = grp

        def quant2(g):
            st[g]["q2"] = quantize(st[g]["grp2"], GROUPS[g][1], "2")

        def mm2(g):
            n = GROUPS[g][1]
            codes, scales = st[g]["q2"]
            banks = []
            for i in range(n):
                bank = psum.tile([P, BANK], F32, name="bank")
                nc.tensor.matmul_mx(
                    out=bank[:],
                    lhsT=codes[:, i * P : (i + 1) * P].bitcast(FP8X4),
                    lhsT_scale=scales[:, i * P : (i + 1) * P],
                    rhs=w1[:].bitcast(FP4X4),
                    rhs_scale=w1_scales[:],
                    start=True,
                    stop=True,
                )
                banks.append(bank)
            st[g]["acc2"] = banks

        def bias(g):
            n = GROUPS[g][1]
            pre = work.tile([P, n, D], F32, name="pre")
            for i in range(n):
                nc.vector.tensor_tensor(out=pre[:, i, :], in0=st[g]["acc2"][i][:], in1=b1_row[:], op=ALU.add)
            st[g]["pre"] = pre

        def gelu(g):
            first, n = GROUPS[g]
            act = work.tile([P, n * D], F32, name="act", bufs=3)
            nc.scalar.activation(out=act[:], in_=st[g]["pre"][:].rearrange("p i d -> p (i d)"), func=ACT.Gelu)
            nc.sync.dma_start(out=u_hbm[:, first * D : (first + n) * D], in_=act[:])

        stages = {"product": product, "turn1": turn1, "copy1": copy1, "quant1": quant1, "mm1": mm1, "zb": zb, "turnb": turnb, "mid": mid, "square": square, "small": small, "norm": norm, "turn2": turn2, "affine": affine, "inter": inter, "quant2": quant2, "mm2": mm2, "bias": bias, "gelu": gelu}
        for step in range(n_groups + max(lag for name, lag in SCHEDULE)):
            for name, lag in SCHEDULE:
                if 0 <= step - lag < n_groups:
                    stages[name](step - lag)
